import numpy as np
import ml_dtypes

BF16 = ml_dtypes.bfloat16


def bf(x):
    return np.asarray(x, np.float32).astype(BF16)


def f32(x):
    return np.asarray(x, np.float32)


def f64(x):
    return np.asarray(x).astype(np.float64)


def striped(idx):
    return np.tile(idx.reshape(-1, 16).T, (8, 1))


Q, S, N, P = 128, 256, 512, 8
LOGIT_SCALE = 5.0
MASK_SCALE = 0.2


def setup_inputs():
    return {"logits": f32(LOGIT_SCALE * np.random.standard_normal((Q, S))), "pred_masks": f32(MASK_SCALE * np.random.random((Q, P))), "tgt_masks": f32(MASK_SCALE * np.random.random((P, N))), "offs": striped(np.random.permutation(np.tile(np.arange(S), 2))[:N])}


def reference(logits, pred_masks, tgt_masks, offs):
    idx = offs[:16].T.reshape(-1)
    z = f64(logits)
    e = np.exp(z - z.max(axis=1, keepdims=True))
    prob = e / e.sum(axis=1, keepdims=True)
    o = f64(pred_masks)[:, :, None]
    t = f64(tgt_masks)[None, :, :]
    l1 = np.abs(o - t).sum(axis=1)
    inter = (o * t).sum(axis=1)
    denom = o.sum(axis=1) + t.sum(axis=1)
    dice = 1.0 - (2.0 * inter + 1.0) / (denom + 1.0)
    return l1 - prob[:, idx] + dice

@@ -1,0 +1,90 @@
+import concourse.mybir as mybir
+from concourse.masks import make_identity
+
+F32 = mybir.dt.float32
+U16 = mybir.dt.uint16
+ALU = mybir.AluOpType
+ACT = mybir.ActivationFunctionType
+AXIS = mybir.AxisListType
+
+Q, S, N, P = 128, 256, 512, 8
+PIECE = S
+FLOPS = 2 * Q * N * P
+
+
+def tile_edlhungarianmatcher_kernel(tc, logits, pred_masks, tgt_masks, offs, out):
+    nc = tc.nc
+    with tc.tile_pool(name="held", bufs=1) as held, tc.psum_pool(name="psum", bufs=1) as psum:
+        offsets = held.tile([Q, N // 16], U16, name="offsets")
+        nc.sync.dma_start(offsets[:], offs)
+        pred = held.tile([Q, P], F32, name="pred")
+        nc.scalar.dma_start(pred[:], pred_masks)
+        tgt = held.tile([P, N], F32, name="tgt")
+        nc.scalar.dma_start(tgt[:], tgt_masks)
+        scores = held.tile([Q, S], F32, name="scores")
+        nc.sync.dma_start(scores[:], logits)
+        tgt_rows = []
+        for n in range(P):
+            row = held.tile([Q, N], F32, name=f"tgt_row{n}")
+            queue = nc.sync if n % 2 == 0 else nc.scalar
+            queue.dma_start(row[:], tgt_masks[n, :].partition_broadcast(Q))
+            tgt_rows.append(row)
+
+        identity = held.tile([Q, Q], F32, name="identity")
+        make_identity(nc, identity[:])
+        ones = held.tile([P, Q], F32, name="ones")
+        nc.gpsimd.memset(ones[:], 1.0)
+
+        neg_max = held.tile([Q, 1], F32, name="neg_max")
+        nc.vector.reduce_max(neg_max[:], scores[:], axis=AXIS.X, negate=True)
+        expd = held.tile([Q, S], F32, name="expd")
+        exp_sum = held.tile([Q, 1], F32, name="exp_sum")
+        nc.scalar.activation(expd[:], scores[:], ACT.Exp, bias=neg_max[:], scale=1.0, accum_out=exp_sum[:])
+        inv_sum = held.tile([Q, 1], F32, name="inv_sum")
+        nc.vector.reciprocal(inv_sum[:], exp_sum[:])
+        neg_prob = held.tile([Q, S], F32, name="neg_prob")
+        nc.vector.tensor_scalar(neg_prob[:], expd[:], inv_sum[:], -1.0, op0=ALU.mult, op1=ALU.mult)
+
+        pred_t_ps = psum.tile([P, Q], F32, name="pred_t_ps")
+        nc.tensor.transpose(pred_t_ps[:], pred[:], identity[:])
+        pred_t = held.tile([P, Q], F32, name="pred_t")
+        nc.scalar.copy(pred_t[:], pred_t_ps[:])
+        tm_ps = psum.tile([Q, N], F32, name="tm_ps")
+        nc.tensor.matmul(tm_ps[:], ones[:], tgt[:], start=True, stop=True)
+        inter_ps = psum.tile([Q, N], F32, name="inter_ps")
+        nc.tensor.matmul(inter_ps[:], pred_t[:], tgt[:], start=True, stop=True)
+
+        pm_plus_1 = held.tile([Q, 1], F32, name="pm_plus_1")
+        nc.vector.reduce_sum(pm_plus_1[:], pred[:], axis=AXIS.X)
+        nc.vector.tensor_scalar_add(pm_plus_1[:], pm_plus_1[:], 1.0)
+        denom = held.tile([Q, N], F32, name="denom")
+        nc.scalar.activation(denom[:], tm_ps[:], ACT.Identity, bias=pm_plus_1[:], scale=1.0)
+        inv_denom = held.tile([Q, N], F32, name="inv_denom")
+        nc.vector.reciprocal(inv_denom[:], denom[:])
+        half_ratio = held.tile([Q, N], F32, name="half_ratio")
+        nc.vector.scalar_tensor_tensor(
+            half_ratio[:], inter_ps[:], 0.5, inv_denom[:], op0=ALU.add, op1=ALU.mult
+        )
+
+        min_sum = held.tile([Q, N], F32, name="min_sum")
+        nc.vector.tensor_scalar(min_sum[:], tgt_rows[0][:], pred[:, 0:1], None, op0=ALU.min)
+        for n in range(1, P):
+            nc.vector.scalar_tensor_tensor(
+                min_sum[:], tgt_rows[n][:], pred[:, n : n + 1], min_sum[:], op0=ALU.min, op1=ALU.add
+            )
+
+        nc.vector.tensor_tensor(min_sum[:], min_sum[:], half_ratio[:], ALU.add)
+        mask_cost = held.tile([Q, N], F32, name="mask_cost")
+        nc.vector.scalar_tensor_tensor(
+            mask_cost[:], min_sum[:], -2.0, denom[:], op0=ALU.mult, op1=ALU.add
+        )
+
+        cost = held.tile([Q, N], F32, name="cost")
+        for piece in range(N // PIECE):
+            columns = slice(piece * PIECE, (piece + 1) * PIECE)
+            piece_offsets = offsets[:, piece * (PIECE // 16) : (piece + 1) * (PIECE // 16)]
+            nc.vector.tensor_tensor(
+                cost[:, columns], neg_prob[:].indirect(piece_offsets), mask_cost[:, columns], ALU.add
+            )
+            queue = nc.sync if piece % 2 == 0 else nc.scalar
+            queue.dma_start(out[:, columns], cost[:, columns])

@@ -34,6 +34,9 @@ def tile_edlhungarianmatcher_kernel(tc, logits, pred_masks, tgt_masks, offs, out
         make_identity(nc, identity[:])
         ones = held.tile([P, Q], F32, name="ones")
         nc.gpsimd.memset(ones[:], 1.0)
+        scratch = held.tile([Q, 1], F32, name="scratch")
+        nc.vector.memset(scratch[:], 0.0)
+        nc.scalar.activation(scratch[:], scratch[:], ACT.Exp)
 
         neg_max = held.tile([Q, 1], F32, name="neg_max")
         nc.vector.reduce_max(neg_max[:], scores[:], axis=AXIS.X, negate=True)
@@ -48,7 +51,7 @@ def tile_edlhungarianmatcher_kernel(tc, logits, pred_masks, tgt_masks, offs, out
         pred_t_ps = psum.tile([P, Q], F32, name="pred_t_ps")
         nc.tensor.transpose(pred_t_ps[:], pred[:], identity[:])
         pred_t = held.tile([P, Q], F32, name="pred_t")
-        nc.scalar.copy(pred_t[:], pred_t_ps[:])
+        nc.vector.tensor_copy(pred_t[:], pred_t_ps[:])
         tm_ps = psum.tile([Q, N], F32, name="tm_ps")
         nc.tensor.matmul(tm_ps[:], ones[:], tgt[:], start=True, stop=True)
         inter_ps = psum.tile([Q, N], F32, name="inter_ps")
@@ -57,14 +60,16 @@ def tile_edlhungarianmatcher_kernel(tc, logits, pred_masks, tgt_masks, offs, out
         pm_plus_1 = held.tile([Q, 1], F32, name="pm_plus_1")
         nc.vector.reduce_sum(pm_plus_1[:], pred[:], axis=AXIS.X)
         nc.vector.tensor_scalar_add(pm_plus_1[:], pm_plus_1[:], 1.0)
+        inv_root = held.tile([Q, N], F32, name="inv_root")
+        nc.scalar.activation(inv_root[:], tm_ps[:], ACT.Abs_reciprocal_sqrt, bias=pm_plus_1[:], scale=1.0)
+        denom_sign = held.tile([Q, N], F32, name="denom_sign")
+        nc.scalar.activation(denom_sign[:], tm_ps[:], ACT.Sign, bias=pm_plus_1[:], scale=1.0)
+        inv_abs = held.tile([Q, N], F32, name="inv_abs")
+        nc.scalar.activation(inv_abs[:], inv_root[:], ACT.Square)
+        inv_denom = held.tile([Q, N], F32, name="inv_denom")
+        nc.gpsimd.tensor_tensor(inv_denom[:], inv_abs[:], denom_sign[:], ALU.mult)
         denom = held.tile([Q, N], F32, name="denom")
         nc.scalar.activation(denom[:], tm_ps[:], ACT.Identity, bias=pm_plus_1[:], scale=1.0)
-        inv_denom = held.tile([Q, N], F32, name="inv_denom")
-        nc.vector.reciprocal(inv_denom[:], denom[:])
-        half_ratio = held.tile([Q, N], F32, name="half_ratio")
-        nc.vector.scalar_tensor_tensor(
-            half_ratio[:], inter_ps[:], 0.5, inv_denom[:], op0=ALU.add, op1=ALU.mult
-        )
 
         min_sum = held.tile([Q, N], F32, name="min_sum")
         nc.vector.tensor_scalar(min_sum[:], tgt_rows[0][:], pred[:, 0:1], None, op0=ALU.min)
@@ -73,6 +78,10 @@ def tile_edlhungarianmatcher_kernel(tc, logits, pred_masks, tgt_masks, offs, out
                 min_sum[:], tgt_rows[n][:], pred[:, n : n + 1], min_sum[:], op0=ALU.min, op1=ALU.add
             )
 
+        half_ratio = held.tile([Q, N], F32, name="half_ratio")
+        nc.vector.scalar_tensor_tensor(
+            half_ratio[:], inter_ps[:], 0.5, inv_denom[:], op0=ALU.add, op1=ALU.mult
+        )
         nc.vector.tensor_tensor(min_sum[:], min_sum[:], half_ratio[:], ALU.add)
         mask_cost = held.tile([Q, N], F32, name="mask_cost")
         nc.vector.scalar_tensor_tensor(

@@ -1,5 +1,4 @@
 import concourse.mybir as mybir
-from concourse.masks import make_identity
 
 F32 = mybir.dt.float32
 U16 = mybir.dt.uint16
@@ -9,34 +8,50 @@ AXIS = mybir.AxisListType
 
 Q, S, N, P = 128, 256, 512, 8
 PIECE = S
+PIECES = N // PIECE
 FLOPS = 2 * Q * N * P
+ROWS_PER_LOAD = 2
 
 
 def tile_edlhungarianmatcher_kernel(tc, logits, pred_masks, tgt_masks, offs, out):
     nc = tc.nc
     with tc.tile_pool(name="held", bufs=1) as held, tc.psum_pool(name="psum", bufs=1) as psum:
-        offsets = held.tile([Q, N // 16], U16, name="offsets")
-        nc.sync.dma_start(offsets[:], offs)
+        scores = held.tile([Q, S], F32, name="scores")
+        nc.scalar.dma_start(scores[:], logits)
         pred = held.tile([Q, P], F32, name="pred")
         nc.scalar.dma_start(pred[:], pred_masks)
         tgt = held.tile([P, N], F32, name="tgt")
-        nc.scalar.dma_start(tgt[:], tgt_masks)
-        scores = held.tile([Q, S], F32, name="scores")
-        nc.sync.dma_start(scores[:], logits)
+        nc.sync.dma_start(tgt[:], tgt_masks)
+        pred_t = held.tile([P, Q], F32, name="pred_t")
+        with nc.allow_non_contiguous_dma(reason="1,024 single elements: a transposing load of 4 KiB"):
+            nc.sync.dma_start(pred_t[:], pred_masks.rearrange("q n -> n q"))
         tgt_rows = []
-        for n in range(P):
-            row = held.tile([Q, N], F32, name=f"tgt_row{n}")
-            queue = nc.sync if n % 2 == 0 else nc.scalar
-            queue.dma_start(row[:], tgt_masks[n, :].partition_broadcast(Q))
-            tgt_rows.append(row)
+        for first in range(0, P, ROWS_PER_LOAD):
+            rows = held.tile([Q, ROWS_PER_LOAD * N], F32, name=f"tgt_rows{first}")
+            source = tgt_masks[first : first + ROWS_PER_LOAD, :].rearrange("n j -> (n j)")
+            nc.sync.dma_start(rows[:], source.partition_broadcast(Q))
+            for r in range(ROWS_PER_LOAD):
+                tgt_rows.append(rows[:, r * N : (r + 1) * N])
+        offsets = held.tile([Q, N // 16], U16, name="offsets")
+        nc.sync.dma_start(offsets[:], offs)
 
-        identity = held.tile([Q, Q], F32, name="identity")
-        make_identity(nc, identity[:])
         ones = held.tile([P, Q], F32, name="ones")
         nc.gpsimd.memset(ones[:], 1.0)
         scratch = held.tile([Q, 1], F32, name="scratch")
         nc.vector.memset(scratch[:], 0.0)
         nc.scalar.activation(scratch[:], scratch[:], ACT.Exp)
+
+        pieces = [slice(k * PIECE, (k + 1) * PIECE) for k in range(PIECES)]
+
+        tm_ps = [psum.tile([Q, PIECE], F32, name=f"tm_ps{k}") for k in range(PIECES)]
+        for k in range(PIECES):
+            nc.tensor.matmul(tm_ps[k][:], ones[:], tgt[:, pieces[k]], start=True, stop=True)
+        inter_ps = [psum.tile([Q, PIECE], F32, name=f"inter_ps{k}") for k in range(PIECES)]
+        for k in range(PIECES):
+            nc.tensor.matmul(inter_ps[k][:], pred_t[:], tgt[:, pieces[k]], start=True, stop=True)
+        pm_plus_1 = held.tile([Q, 1], F32, name="pm_plus_1")
+        nc.vector.reduce_sum(pm_plus_1[:], pred[:], axis=AXIS.X)
+        nc.vector.tensor_scalar_add(pm_plus_1[:], pm_plus_1[:], 1.0)
 
         neg_max = held.tile([Q, 1], F32, name="neg_max")
         nc.vector.reduce_max(neg_max[:], scores[:], axis=AXIS.X, negate=True)
@@ -48,52 +63,49 @@ def tile_edlhungarianmatcher_kernel(tc, logits, pred_masks, tgt_masks, offs, out
         neg_prob = held.tile([Q, S], F32, name="neg_prob")
         nc.vector.tensor_scalar(neg_prob[:], expd[:], inv_sum[:], -1.0, op0=ALU.mult, op1=ALU.mult)
 
-        pred_t_ps = psum.tile([P, Q], F32, name="pred_t_ps")
-        nc.tensor.transpose(pred_t_ps[:], pred[:], identity[:])
-        pred_t = held.tile([P, Q], F32, name="pred_t")
-        nc.vector.tensor_copy(pred_t[:], pred_t_ps[:])
-        tm_ps = psum.tile([Q, N], F32, name="tm_ps")
-        nc.tensor.matmul(tm_ps[:], ones[:], tgt[:], start=True, stop=True)
-        inter_ps = psum.tile([Q, N], F32, name="inter_ps")
-        nc.tensor.matmul(inter_ps[:], pred_t[:], tgt[:], start=True, stop=True)
-
-        pm_plus_1 = held.tile([Q, 1], F32, name="pm_plus_1")
-        nc.vector.reduce_sum(pm_plus_1[:], pred[:], axis=AXIS.X)
-        nc.vector.tensor_scalar_add(pm_plus_1[:], pm_plus_1[:], 1.0)
-        inv_root = held.tile([Q, N], F32, name="inv_root")
-        nc.scalar.activation(inv_root[:], tm_ps[:], ACT.Abs_reciprocal_sqrt, bias=pm_plus_1[:], scale=1.0)
-        denom_sign = held.tile([Q, N], F32, name="denom_sign")
-        nc.scalar.activation(denom_sign[:], tm_ps[:], ACT.Sign, bias=pm_plus_1[:], scale=1.0)
-        inv_abs = held.tile([Q, N], F32, name="inv_abs")
-        nc.scalar.activation(inv_abs[:], inv_root[:], ACT.Square)
-        inv_denom = held.tile([Q, N], F32, name="inv_denom")
-        nc.gpsimd.tensor_tensor(inv_denom[:], inv_abs[:], denom_sign[:], ALU.mult)
         denom = held.tile([Q, N], F32, name="denom")
-        nc.scalar.activation(denom[:], tm_ps[:], ACT.Identity, bias=pm_plus_1[:], scale=1.0)
+        denom_sign = held.tile([Q, N], F32, name="denom_sign")
+        inv_abs = held.tile([Q, N], F32, name="inv_abs")
+        for k in range(PIECES):
+            piece = pieces[k]
+            nc.vector.tensor_scalar(denom[:, piece], tm_ps[k][:], pm_plus_1[:], None, op0=ALU.add)
+            nc.scalar.activation(inv_abs[:, piece], tm_ps[k][:], ACT.Abs_reciprocal_sqrt, bias=pm_plus_1[:], scale=1.0)
+            nc.scalar.activation(inv_abs[:, piece], inv_abs[:, piece], ACT.Square)
+            nc.scalar.activation(denom_sign[:, piece], tm_ps[k][:], ACT.Sign, bias=pm_plus_1[:], scale=1.0)
+        dice_part = held.tile([Q, N], F32, name="dice_part")
+        for k in range(PIECES):
+            piece = pieces[k]
+            nc.vector.scalar_tensor_tensor(
+                dice_part[:, piece], inter_ps[k][:], 0.5, denom_sign[:, piece], op0=ALU.add, op1=ALU.mult
+            )
+            nc.vector.tensor_tensor(dice_part[:, piece], dice_part[:, piece], inv_abs[:, piece], ALU.mult)
+            nc.vector.scalar_tensor_tensor(
+                dice_part[:, piece], dice_part[:, piece], -2.0, denom[:, piece], op0=ALU.mult, op1=ALU.add
+            )
 
         min_sum = held.tile([Q, N], F32, name="min_sum")
-        nc.vector.tensor_scalar(min_sum[:], tgt_rows[0][:], pred[:, 0:1], None, op0=ALU.min)
-        for n in range(1, P):
-            nc.vector.scalar_tensor_tensor(
-                min_sum[:], tgt_rows[n][:], pred[:, n : n + 1], min_sum[:], op0=ALU.min, op1=ALU.add
-            )
+        for n in range(P):
+            for piece in pieces:
+                if n == 0:
+                    nc.vector.tensor_scalar(
+                        min_sum[:, piece], tgt_rows[n][:, piece], pred[:, n : n + 1], None, op0=ALU.min
+                    )
+                else:
+                    nc.vector.scalar_tensor_tensor(
+                        min_sum[:, piece], tgt_rows[n][:, piece], pred[:, n : n + 1], min_sum[:, piece],
+                        op0=ALU.min, op1=ALU.add,
+                    )
 
-        half_ratio = held.tile([Q, N], F32, name="half_ratio")
-        nc.vector.scalar_tensor_tensor(
-            half_ratio[:], inter_ps[:], 0.5, inv_denom[:], op0=ALU.add, op1=ALU.mult
-        )
-        nc.vector.tensor_tensor(min_sum[:], min_sum[:], half_ratio[:], ALU.add)
         mask_cost = held.tile([Q, N], F32, name="mask_cost")
-        nc.vector.scalar_tensor_tensor(
-            mask_cost[:], min_sum[:], -2.0, denom[:], op0=ALU.mult, op1=ALU.add
-        )
-
         cost = held.tile([Q, N], F32, name="cost")
-        for piece in range(N // PIECE):
-            columns = slice(piece * PIECE, (piece + 1) * PIECE)
-            piece_offsets = offsets[:, piece * (PIECE // 16) : (piece + 1) * (PIECE // 16)]
-            nc.vector.tensor_tensor(
-                cost[:, columns], neg_prob[:].indirect(piece_offsets), mask_cost[:, columns], ALU.add
+        for k in range(PIECES):
+            piece = pieces[k]
+            nc.vector.scalar_tensor_tensor(
+                mask_cost[:, piece], min_sum[:, piece], -2.0, dice_part[:, piece], op0=ALU.mult, op1=ALU.add
             )
-            queue = nc.sync if piece % 2 == 0 else nc.scalar
-            queue.dma_start(out[:, columns], cost[:, columns])
+            piece_offsets = offsets[:, k * (PIECE // 16) : (k + 1) * (PIECE // 16)]
+            nc.vector.tensor_tensor(
+                cost[:, piece], neg_prob[:].indirect(piece_offsets), mask_cost[:, piece], ALU.add
+            )
+            queue = nc.sync if k % 2 == 0 else nc.scalar
+            queue.dma_start(out[:, piece], cost[:, piece])

@@ -10,7 +10,6 @@ Q, S, N, P = 128, 256, 512, 8
 PIECE = S
 PIECES = N // PIECE
 FLOPS = 2 * Q * N * P
-ROWS_PER_LOAD = 2
 
 
 def tile_edlhungarianmatcher_kernel(tc, logits, pred_masks, tgt_masks, offs, out):
@@ -20,25 +19,23 @@ def tile_edlhungarianmatcher_kernel(tc, logits, pred_masks, tgt_masks, offs, out
         nc.scalar.dma_start(scores[:], logits)
         pred = held.tile([Q, P], F32, name="pred")
         nc.scalar.dma_start(pred[:], pred_masks)
-        tgt = held.tile([P, N], F32, name="tgt")
-        nc.sync.dma_start(tgt[:], tgt_masks)
         pred_t = held.tile([P, Q], F32, name="pred_t")
         with nc.allow_non_contiguous_dma(reason="1,024 single elements: a transposing load of 4 KiB"):
-            nc.sync.dma_start(pred_t[:], pred_masks.rearrange("q n -> n q"))
+            nc.scalar.dma_start(pred_t[:], pred_masks.rearrange("q n -> n q"))
+        tgt = held.tile([P, N], F32, name="tgt")
+        nc.sync.dma_start(tgt[:], tgt_masks)
         tgt_rows = []
-        for first in range(0, P, ROWS_PER_LOAD):
-            rows = held.tile([Q, ROWS_PER_LOAD * N], F32, name=f"tgt_rows{first}")
-            source = tgt_masks[first : first + ROWS_PER_LOAD, :].rearrange("n j -> (n j)")
-            nc.sync.dma_start(rows[:], source.partition_broadcast(Q))
-            for r in range(ROWS_PER_LOAD):
-                tgt_rows.append(rows[:, r * N : (r + 1) * N])
+        for n in range(P):
+            row = held.tile([Q, N], F32, name=f"tgt_row{n}")
+            nc.sync.dma_start(row[:], tgt_masks[n, :].partition_broadcast(Q))
+            tgt_rows.append(row)
         offsets = held.tile([Q, N // 16], U16, name="offsets")
         nc.sync.dma_start(offsets[:], offs)
 
         ones = held.tile([P, Q], F32, name="ones")
         nc.gpsimd.memset(ones[:], 1.0)
         scratch = held.tile([Q, 1], F32, name="scratch")
-        nc.vector.memset(scratch[:], 0.0)
+        nc.gpsimd.memset(scratch[:], 0.0)
         nc.scalar.activation(scratch[:], scratch[:], ACT.Exp)
 
         pieces = [slice(k * PIECE, (k + 1) * PIECE) for k in range(PIECES)]
@@ -61,24 +58,26 @@ def tile_edlhungarianmatcher_kernel(tc, logits, pred_masks, tgt_masks, offs, out
         inv_sum = held.tile([Q, 1], F32, name="inv_sum")
         nc.vector.reciprocal(inv_sum[:], exp_sum[:])
         neg_prob = held.tile([Q, S], F32, name="neg_prob")
-        nc.vector.tensor_scalar(neg_prob[:], expd[:], inv_sum[:], -1.0, op0=ALU.mult, op1=ALU.mult)
+        nc.gpsimd.tensor_scalar(neg_prob[:], expd[:], inv_sum[:], -1.0, op0=ALU.mult, op1=ALU.mult)
 
         denom = held.tile([Q, N], F32, name="denom")
         denom_sign = held.tile([Q, N], F32, name="denom_sign")
         inv_abs = held.tile([Q, N], F32, name="inv_abs")
+        inv_denom = held.tile([Q, N], F32, name="inv_denom")
         for k in range(PIECES):
             piece = pieces[k]
-            nc.vector.tensor_scalar(denom[:, piece], tm_ps[k][:], pm_plus_1[:], None, op0=ALU.add)
             nc.scalar.activation(inv_abs[:, piece], tm_ps[k][:], ACT.Abs_reciprocal_sqrt, bias=pm_plus_1[:], scale=1.0)
             nc.scalar.activation(inv_abs[:, piece], inv_abs[:, piece], ACT.Square)
             nc.scalar.activation(denom_sign[:, piece], tm_ps[k][:], ACT.Sign, bias=pm_plus_1[:], scale=1.0)
+            nc.gpsimd.tensor_tensor(inv_denom[:, piece], inv_abs[:, piece], denom_sign[:, piece], ALU.mult)
+        for k in range(PIECES):
+            nc.scalar.activation(denom[:, pieces[k]], tm_ps[k][:], ACT.Identity, bias=pm_plus_1[:], scale=1.0)
         dice_part = held.tile([Q, N], F32, name="dice_part")
         for k in range(PIECES):
             piece = pieces[k]
             nc.vector.scalar_tensor_tensor(
-                dice_part[:, piece], inter_ps[k][:], 0.5, denom_sign[:, piece], op0=ALU.add, op1=ALU.mult
+                dice_part[:, piece], inter_ps[k][:], 0.5, inv_denom[:, piece], op0=ALU.add, op1=ALU.mult
             )
-            nc.vector.tensor_tensor(dice_part[:, piece], dice_part[:, piece], inv_abs[:, piece], ALU.mult)
             nc.vector.scalar_tensor_tensor(
                 dice_part[:, piece], dice_part[:, piece], -2.0, denom[:, piece], op0=ALU.mult, op1=ALU.add
             )

@@ -58,26 +58,24 @@ def tile_edlhungarianmatcher_kernel(tc, logits, pred_masks, tgt_masks, offs, out
         inv_sum = held.tile([Q, 1], F32, name="inv_sum")
         nc.vector.reciprocal(inv_sum[:], exp_sum[:])
         neg_prob = held.tile([Q, S], F32, name="neg_prob")
-        nc.gpsimd.tensor_scalar(neg_prob[:], expd[:], inv_sum[:], -1.0, op0=ALU.mult, op1=ALU.mult)
+        nc.vector.tensor_scalar(neg_prob[:], expd[:], inv_sum[:], -1.0, op0=ALU.mult, op1=ALU.mult)
 
         denom = held.tile([Q, N], F32, name="denom")
         denom_sign = held.tile([Q, N], F32, name="denom_sign")
         inv_abs = held.tile([Q, N], F32, name="inv_abs")
-        inv_denom = held.tile([Q, N], F32, name="inv_denom")
         for k in range(PIECES):
             piece = pieces[k]
             nc.scalar.activation(inv_abs[:, piece], tm_ps[k][:], ACT.Abs_reciprocal_sqrt, bias=pm_plus_1[:], scale=1.0)
             nc.scalar.activation(inv_abs[:, piece], inv_abs[:, piece], ACT.Square)
             nc.scalar.activation(denom_sign[:, piece], tm_ps[k][:], ACT.Sign, bias=pm_plus_1[:], scale=1.0)
-            nc.gpsimd.tensor_tensor(inv_denom[:, piece], inv_abs[:, piece], denom_sign[:, piece], ALU.mult)
-        for k in range(PIECES):
-            nc.scalar.activation(denom[:, pieces[k]], tm_ps[k][:], ACT.Identity, bias=pm_plus_1[:], scale=1.0)
+            nc.scalar.activation(denom[:, piece], tm_ps[k][:], ACT.Identity, bias=pm_plus_1[:], scale=1.0)
         dice_part = held.tile([Q, N], F32, name="dice_part")
         for k in range(PIECES):
             piece = pieces[k]
             nc.vector.scalar_tensor_tensor(
-                dice_part[:, piece], inter_ps[k][:], 0.5, inv_denom[:, piece], op0=ALU.add, op1=ALU.mult
+                dice_part[:, piece], inter_ps[k][:], 0.5, denom_sign[:, piece], op0=ALU.add, op1=ALU.mult
             )
+            nc.vector.tensor_tensor(dice_part[:, piece], dice_part[:, piece], inv_abs[:, piece], ALU.mult)
             nc.vector.scalar_tensor_tensor(
                 dice_part[:, piece], dice_part[:, piece], -2.0, denom[:, piece], op0=ALU.mult, op1=ALU.add
             )

@@ -10,6 +10,7 @@ Q, S, N, P = 128, 256, 512, 8
 PIECE = S
 PIECES = N // PIECE
 FLOPS = 2 * Q * N * P
+ROWS_PER_LOAD = 2
 
 
 def tile_edlhungarianmatcher_kernel(tc, logits, pred_masks, tgt_masks, offs, out):
@@ -19,16 +20,19 @@ def tile_edlhungarianmatcher_kernel(tc, logits, pred_masks, tgt_masks, offs, out
         nc.scalar.dma_start(scores[:], logits)
         pred = held.tile([Q, P], F32, name="pred")
         nc.scalar.dma_start(pred[:], pred_masks)
-        pred_t = held.tile([P, Q], F32, name="pred_t")
-        with nc.allow_non_contiguous_dma(reason="1,024 single elements: a transposing load of 4 KiB"):
-            nc.scalar.dma_start(pred_t[:], pred_masks.rearrange("q n -> n q"))
         tgt = held.tile([P, N], F32, name="tgt")
         nc.sync.dma_start(tgt[:], tgt_masks)
         tgt_rows = []
-        for n in range(P):
-            row = held.tile([Q, N], F32, name=f"tgt_row{n}")
-            nc.sync.dma_start(row[:], tgt_masks[n, :].partition_broadcast(Q))
-            tgt_rows.append(row)
+        pred_t = held.tile([P, Q], F32, name="pred_t")
+        for first in range(0, P, ROWS_PER_LOAD):
+            if first == P // 2:
+                with nc.allow_non_contiguous_dma(reason="1,024 single elements: a transposing load of 4 KiB"):
+                    nc.sync.dma_start(pred_t[:], pred_masks.rearrange("q n -> n q"))
+            rows = held.tile([Q, ROWS_PER_LOAD * N], F32, name=f"tgt_rows{first}")
+            source = tgt_masks[first : first + ROWS_PER_LOAD, :].rearrange("n j -> (n j)")
+            nc.sync.dma_start(rows[:], source.partition_broadcast(Q))
+            for r in range(ROWS_PER_LOAD):
+                tgt_rows.append(rows[:, r * N : (r + 1) * N])
         offsets = held.tile([Q, N // 16], U16, name="offsets")
         nc.sync.dma_start(offsets[:], offs)
 
@@ -58,24 +62,26 @@ def tile_edlhungarianmatcher_kernel(tc, logits, pred_masks, tgt_masks, offs, out
         inv_sum = held.tile([Q, 1], F32, name="inv_sum")
         nc.vector.reciprocal(inv_sum[:], exp_sum[:])
         neg_prob = held.tile([Q, S], F32, name="neg_prob")
-        nc.vector.tensor_scalar(neg_prob[:], expd[:], inv_sum[:], -1.0, op0=ALU.mult, op1=ALU.mult)
+        nc.gpsimd.tensor_scalar(neg_prob[:], expd[:], inv_sum[:], -1.0, op0=ALU.mult, op1=ALU.mult)
 
         denom = held.tile([Q, N], F32, name="denom")
         denom_sign = held.tile([Q, N], F32, name="denom_sign")
         inv_abs = held.tile([Q, N], F32, name="inv_abs")
+        inv_denom = held.tile([Q, N], F32, name="inv_denom")
         for k in range(PIECES):
             piece = pieces[k]
             nc.scalar.activation(inv_abs[:, piece], tm_ps[k][:], ACT.Abs_reciprocal_sqrt, bias=pm_plus_1[:], scale=1.0)
             nc.scalar.activation(inv_abs[:, piece], inv_abs[:, piece], ACT.Square)
             nc.scalar.activation(denom_sign[:, piece], tm_ps[k][:], ACT.Sign, bias=pm_plus_1[:], scale=1.0)
-            nc.scalar.activation(denom[:, piece], tm_ps[k][:], ACT.Identity, bias=pm_plus_1[:], scale=1.0)
+            nc.gpsimd.tensor_tensor(inv_denom[:, piece], inv_abs[:, piece], denom_sign[:, piece], ALU.mult)
+        for k in range(PIECES):
+            nc.scalar.activation(denom[:, pieces[k]], tm_ps[k][:], ACT.Identity, bias=pm_plus_1[:], scale=1.0)
         dice_part = held.tile([Q, N], F32, name="dice_part")
         for k in range(PIECES):
             piece = pieces[k]
             nc.vector.scalar_tensor_tensor(
-                dice_part[:, piece], inter_ps[k][:], 0.5, denom_sign[:, piece], op0=ALU.add, op1=ALU.mult
+                dice_part[:, piece], inter_ps[k][:], 0.5, inv_denom[:, piece], op0=ALU.add, op1=ALU.mult
             )
-            nc.vector.tensor_tensor(dice_part[:, piece], dice_part[:, piece], inv_abs[:, piece], ALU.mult)
             nc.vector.scalar_tensor_tensor(
                 dice_part[:, piece], dice_part[:, piece], -2.0, denom[:, piece], op0=ALU.mult, op1=ALU.add
             )

@@ -37,9 +37,9 @@ def tile_edlhungarianmatcher_kernel(tc, logits, pred_masks, tgt_masks, offs, out
         nc.sync.dma_start(offsets[:], offs)
 
         ones = held.tile([P, Q], F32, name="ones")
-        nc.gpsimd.memset(ones[:], 1.0)
+        nc.vector.memset(ones[:], 1.0)
         scratch = held.tile([Q, 1], F32, name="scratch")
-        nc.gpsimd.memset(scratch[:], 0.0)
+        nc.vector.memset(scratch[:], 0.0)
         nc.scalar.activation(scratch[:], scratch[:], ACT.Exp)
 
         pieces = [slice(k * PIECE, (k + 1) * PIECE) for k in range(PIECES)]

@@ -22,12 +22,11 @@ def tile_edlhungarianmatcher_kernel(tc, logits, pred_masks, tgt_masks, offs, out
         nc.scalar.dma_start(pred[:], pred_masks)
         tgt = held.tile([P, N], F32, name="tgt")
         nc.sync.dma_start(tgt[:], tgt_masks)
-        tgt_rows = []
         pred_t = held.tile([P, Q], F32, name="pred_t")
+        with nc.allow_non_contiguous_dma(reason="1,024 single elements: a transposing load of 4 KiB"):
+            nc.sync.dma_start(pred_t[:], pred_masks.rearrange("q n -> n q"))
+        tgt_rows = []
         for first in range(0, P, ROWS_PER_LOAD):
-            if first == P // 2:
-                with nc.allow_non_contiguous_dma(reason="1,024 single elements: a transposing load of 4 KiB"):
-                    nc.sync.dma_start(pred_t[:], pred_masks.rearrange("q n -> n q"))
             rows = held.tile([Q, ROWS_PER_LOAD * N], F32, name=f"tgt_rows{first}")
             source = tgt_masks[first : first + ROWS_PER_LOAD, :].rearrange("n j -> (n j)")
             nc.sync.dma_start(rows[:], source.partition_broadcast(Q))
@@ -37,7 +36,7 @@ def tile_edlhungarianmatcher_kernel(tc, logits, pred_masks, tgt_masks, offs, out
         nc.sync.dma_start(offsets[:], offs)
 
         ones = held.tile([P, Q], F32, name="ones")
-        nc.vector.memset(ones[:], 1.0)
+        nc.gpsimd.memset(ones[:], 1.0)
         scratch = held.tile([Q, 1], F32, name="scratch")
         nc.vector.memset(scratch[:], 0.0)
         nc.scalar.activation(scratch[:], scratch[:], ACT.Exp)
@@ -70,12 +69,11 @@ def tile_edlhungarianmatcher_kernel(tc, logits, pred_masks, tgt_masks, offs, out
         inv_denom = held.tile([Q, N], F32, name="inv_denom")
         for k in range(PIECES):
             piece = pieces[k]
+            nc.vector.tensor_scalar(denom[:, piece], tm_ps[k][:], pm_plus_1[:], None, op0=ALU.add)
             nc.scalar.activation(inv_abs[:, piece], tm_ps[k][:], ACT.Abs_reciprocal_sqrt, bias=pm_plus_1[:], scale=1.0)
             nc.scalar.activation(inv_abs[:, piece], inv_abs[:, piece], ACT.Square)
             nc.scalar.activation(denom_sign[:, piece], tm_ps[k][:], ACT.Sign, bias=pm_plus_1[:], scale=1.0)
             nc.gpsimd.tensor_tensor(inv_denom[:, piece], inv_abs[:, piece], denom_sign[:, piece], ALU.mult)
-        for k in range(PIECES):
-            nc.scalar.activation(denom[:, pieces[k]], tm_ps[k][:], ACT.Identity, bias=pm_plus_1[:], scale=1.0)
         dice_part = held.tile([Q, N], F32, name="dice_part")
         for k in range(PIECES):
             piece = pieces[k]

@@ -61,19 +61,16 @@ def tile_edlhungarianmatcher_kernel(tc, logits, pred_masks, tgt_masks, offs, out
         inv_sum = held.tile([Q, 1], F32, name="inv_sum")
         nc.vector.reciprocal(inv_sum[:], exp_sum[:])
         neg_prob = held.tile([Q, S], F32, name="neg_prob")
-        nc.gpsimd.tensor_scalar(neg_prob[:], expd[:], inv_sum[:], -1.0, op0=ALU.mult, op1=ALU.mult)
+        nc.vector.tensor_scalar(neg_prob[:], expd[:], inv_sum[:], -1.0, op0=ALU.mult, op1=ALU.mult)
 
         denom = held.tile([Q, N], F32, name="denom")
-        denom_sign = held.tile([Q, N], F32, name="denom_sign")
-        inv_abs = held.tile([Q, N], F32, name="inv_abs")
+        inv_root = held.tile([Q, N], F32, name="inv_root")
         inv_denom = held.tile([Q, N], F32, name="inv_denom")
         for k in range(PIECES):
             piece = pieces[k]
             nc.vector.tensor_scalar(denom[:, piece], tm_ps[k][:], pm_plus_1[:], None, op0=ALU.add)
-            nc.scalar.activation(inv_abs[:, piece], tm_ps[k][:], ACT.Abs_reciprocal_sqrt, bias=pm_plus_1[:], scale=1.0)
-            nc.scalar.activation(inv_abs[:, piece], inv_abs[:, piece], ACT.Square)
-            nc.scalar.activation(denom_sign[:, piece], tm_ps[k][:], ACT.Sign, bias=pm_plus_1[:], scale=1.0)
-            nc.gpsimd.tensor_tensor(inv_denom[:, piece], inv_abs[:, piece], denom_sign[:, piece], ALU.mult)
+            nc.scalar.activation(inv_root[:, piece], tm_ps[k][:], ACT.Abs_reciprocal_sqrt, bias=pm_plus_1[:], scale=1.0)
+            nc.scalar.activation(inv_denom[:, piece], inv_root[:, piece], ACT.Square)
         dice_part = held.tile([Q, N], F32, name="dice_part")
         for k in range(PIECES):
             piece = pieces[k]

@@ -46,12 +46,15 @@ def tile_edlhungarianmatcher_kernel(tc, logits, pred_masks, tgt_masks, offs, out
         tm_ps = [psum.tile([Q, PIECE], F32, name=f"tm_ps{k}") for k in range(PIECES)]
         for k in range(PIECES):
             nc.tensor.matmul(tm_ps[k][:], ones[:], tgt[:, pieces[k]], start=True, stop=True)
-        inter_ps = [psum.tile([Q, PIECE], F32, name=f"inter_ps{k}") for k in range(PIECES)]
+        weights = held.tile([P, Q], F32, name="weights")
+        nc.vector.tensor_scalar(weights[:], pred_t[:], -2.0, 1.0, op0=ALU.mult, op1=ALU.add)
+        tm_less_2inter_ps = [psum.tile([Q, PIECE], F32, name=f"tm_less_2inter_ps{k}") for k in range(PIECES)]
         for k in range(PIECES):
-            nc.tensor.matmul(inter_ps[k][:], pred_t[:], tgt[:, pieces[k]], start=True, stop=True)
+            nc.tensor.matmul(tm_less_2inter_ps[k][:], weights[:], tgt[:, pieces[k]], start=True, stop=True)
+        pm = held.tile([Q, 1], F32, name="pm")
+        nc.vector.reduce_sum(pm[:], pred[:], axis=AXIS.X)
         pm_plus_1 = held.tile([Q, 1], F32, name="pm_plus_1")
-        nc.vector.reduce_sum(pm_plus_1[:], pred[:], axis=AXIS.X)
-        nc.vector.tensor_scalar_add(pm_plus_1[:], pm_plus_1[:], 1.0)
+        nc.vector.tensor_scalar_add(pm_plus_1[:], pm[:], 1.0)
 
         neg_max = held.tile([Q, 1], F32, name="neg_max")
         nc.vector.reduce_max(neg_max[:], scores[:], axis=AXIS.X, negate=True)
@@ -63,22 +66,21 @@ def tile_edlhungarianmatcher_kernel(tc, logits, pred_masks, tgt_masks, offs, out
         neg_prob = held.tile([Q, S], F32, name="neg_prob")
         nc.vector.tensor_scalar(neg_prob[:], expd[:], inv_sum[:], -1.0, op0=ALU.mult, op1=ALU.mult)
 
-        denom = held.tile([Q, N], F32, name="denom")
         inv_root = held.tile([Q, N], F32, name="inv_root")
         inv_denom = held.tile([Q, N], F32, name="inv_denom")
+        dice = held.tile([Q, N], F32, name="dice")
+        rest = held.tile([Q, N], F32, name="rest")
         for k in range(PIECES):
             piece = pieces[k]
-            nc.vector.tensor_scalar(denom[:, piece], tm_ps[k][:], pm_plus_1[:], None, op0=ALU.add)
             nc.scalar.activation(inv_root[:, piece], tm_ps[k][:], ACT.Abs_reciprocal_sqrt, bias=pm_plus_1[:], scale=1.0)
             nc.scalar.activation(inv_denom[:, piece], inv_root[:, piece], ACT.Square)
-        dice_part = held.tile([Q, N], F32, name="dice_part")
         for k in range(PIECES):
             piece = pieces[k]
             nc.vector.scalar_tensor_tensor(
-                dice_part[:, piece], inter_ps[k][:], 0.5, inv_denom[:, piece], op0=ALU.add, op1=ALU.mult
+                dice[:, piece], tm_less_2inter_ps[k][:], pm[:], inv_denom[:, piece], op0=ALU.add, op1=ALU.mult
             )
             nc.vector.scalar_tensor_tensor(
-                dice_part[:, piece], dice_part[:, piece], -2.0, denom[:, piece], op0=ALU.mult, op1=ALU.add
+                rest[:, piece], tm_ps[k][:], pm[:], dice[:, piece], op0=ALU.add, op1=ALU.add
             )
 
         min_sum = held.tile([Q, N], F32, name="min_sum")
@@ -99,7 +101,7 @@ def tile_edlhungarianmatcher_kernel(tc, logits, pred_masks, tgt_masks, offs, out
         for k in range(PIECES):
             piece = pieces[k]
             nc.vector.scalar_tensor_tensor(
-                mask_cost[:, piece], min_sum[:, piece], -2.0, dice_part[:, piece], op0=ALU.mult, op1=ALU.add
+                mask_cost[:, piece], min_sum[:, piece], -2.0, rest[:, piece], op0=ALU.mult, op1=ALU.add
             )
             piece_offsets = offsets[:, k * (PIECE // 16) : (k + 1) * (PIECE // 16)]
             nc.vector.tensor_tensor(

@@ -1,4 +1,5 @@
 import concourse.mybir as mybir
+from concourse.masks import make_identity
 
 F32 = mybir.dt.float32
 U16 = mybir.dt.uint16
@@ -19,12 +20,9 @@ def tile_edlhungarianmatcher_kernel(tc, logits, pred_masks, tgt_masks, offs, out
         scores = held.tile([Q, S], F32, name="scores")
         nc.scalar.dma_start(scores[:], logits)
         pred = held.tile([Q, P], F32, name="pred")
-        nc.scalar.dma_start(pred[:], pred_masks)
+        nc.sync.dma_start(pred[:], pred_masks)
         tgt = held.tile([P, N], F32, name="tgt")
         nc.sync.dma_start(tgt[:], tgt_masks)
-        pred_t = held.tile([P, Q], F32, name="pred_t")
-        with nc.allow_non_contiguous_dma(reason="1,024 single elements: a transposing load of 4 KiB"):
-            nc.sync.dma_start(pred_t[:], pred_masks.rearrange("q n -> n q"))
         tgt_rows = []
         for first in range(0, P, ROWS_PER_LOAD):
             rows = held.tile([Q, ROWS_PER_LOAD * N], F32, name=f"tgt_rows{first}")
@@ -37,17 +35,21 @@ def tile_edlhungarianmatcher_kernel(tc, logits, pred_masks, tgt_masks, offs, out
 
         ones = held.tile([P, Q], F32, name="ones")
         nc.gpsimd.memset(ones[:], 1.0)
+        identity = held.tile([Q, Q], F32, name="identity")
+        make_identity(nc, identity[:])
         scratch = held.tile([Q, 1], F32, name="scratch")
         nc.vector.memset(scratch[:], 0.0)
         nc.scalar.activation(scratch[:], scratch[:], ACT.Exp)
 
         pieces = [slice(k * PIECE, (k + 1) * PIECE) for k in range(PIECES)]
 
+        pred_t_ps = psum.tile([P, Q], F32, name="pred_t_ps")
+        nc.tensor.transpose(pred_t_ps[:], pred[:], identity[:])
+        weights = held.tile([P, Q], F32, name="weights")
+        nc.scalar.activation(weights[:], pred_t_ps[:], ACT.Identity, bias=1.0, scale=-2.0)
         tm_ps = [psum.tile([Q, PIECE], F32, name=f"tm_ps{k}") for k in range(PIECES)]
         for k in range(PIECES):
             nc.tensor.matmul(tm_ps[k][:], ones[:], tgt[:, pieces[k]], start=True, stop=True)
-        weights = held.tile([P, Q], F32, name="weights")
-        nc.vector.tensor_scalar(weights[:], pred_t[:], -2.0, 1.0, op0=ALU.mult, op1=ALU.add)
         tm_less_2inter_ps = [psum.tile([Q, PIECE], F32, name=f"tm_less_2inter_ps{k}") for k in range(PIECES)]
         for k in range(PIECES):
             nc.tensor.matmul(tm_less_2inter_ps[k][:], weights[:], tgt[:, pieces[k]], start=True, stop=True)
@@ -68,19 +70,18 @@ def tile_edlhungarianmatcher_kernel(tc, logits, pred_masks, tgt_masks, offs, out
 
         inv_root = held.tile([Q, N], F32, name="inv_root")
         inv_denom = held.tile([Q, N], F32, name="inv_denom")
-        dice = held.tile([Q, N], F32, name="dice")
-        rest = held.tile([Q, N], F32, name="rest")
+        mask_sums = held.tile([Q, N], F32, name="mask_sums")
         for k in range(PIECES):
             piece = pieces[k]
             nc.scalar.activation(inv_root[:, piece], tm_ps[k][:], ACT.Abs_reciprocal_sqrt, bias=pm_plus_1[:], scale=1.0)
             nc.scalar.activation(inv_denom[:, piece], inv_root[:, piece], ACT.Square)
+            nc.scalar.activation(mask_sums[:, piece], tm_ps[k][:], ACT.Identity, bias=pm[:], scale=1.0)
+
+        picked = held.tile([Q, N], F32, name="picked")
         for k in range(PIECES):
-            piece = pieces[k]
-            nc.vector.scalar_tensor_tensor(
-                dice[:, piece], tm_less_2inter_ps[k][:], pm[:], inv_denom[:, piece], op0=ALU.add, op1=ALU.mult
-            )
-            nc.vector.scalar_tensor_tensor(
-                rest[:, piece], tm_ps[k][:], pm[:], dice[:, piece], op0=ALU.add, op1=ALU.add
+            piece_offsets = offsets[:, k * (PIECE // 16) : (k + 1) * (PIECE // 16)]
+            nc.vector.tensor_tensor(
+                picked[:, pieces[k]], neg_prob[:].indirect(piece_offsets), mask_sums[:, pieces[k]], ALU.add
             )
 
         min_sum = held.tile([Q, N], F32, name="min_sum")
@@ -96,16 +97,17 @@ def tile_edlhungarianmatcher_kernel(tc, logits, pred_masks, tgt_masks, offs, out
                         op0=ALU.min, op1=ALU.add,
                     )
 
-        mask_cost = held.tile([Q, N], F32, name="mask_cost")
+        no_dice = held.tile([Q, N], F32, name="no_dice")
+        dice = held.tile([Q, N], F32, name="dice")
         cost = held.tile([Q, N], F32, name="cost")
         for k in range(PIECES):
             piece = pieces[k]
             nc.vector.scalar_tensor_tensor(
-                mask_cost[:, piece], min_sum[:, piece], -2.0, rest[:, piece], op0=ALU.mult, op1=ALU.add
+                dice[:, piece], tm_less_2inter_ps[k][:], pm[:], inv_denom[:, piece], op0=ALU.add, op1=ALU.mult
             )
-            piece_offsets = offsets[:, k * (PIECE // 16) : (k + 1) * (PIECE // 16)]
-            nc.vector.tensor_tensor(
-                cost[:, piece], neg_prob[:].indirect(piece_offsets), mask_cost[:, piece], ALU.add
+            nc.vector.scalar_tensor_tensor(
+                no_dice[:, piece], min_sum[:, piece], -2.0, picked[:, piece], op0=ALU.mult, op1=ALU.add
             )
+            nc.vector.tensor_tensor(cost[:, piece], no_dice[:, piece], dice[:, piece], ALU.add)
             queue = nc.sync if k % 2 == 0 else nc.scalar
             queue.dma_start(out[:, piece], cost[:, piece])

@@ -12,6 +12,7 @@ PIECE = S
 PIECES = N // PIECE
 FLOPS = 2 * Q * N * P
 ROWS_PER_LOAD = 2
+LAST_PIECE = 128
 
 
 def tile_edlhungarianmatcher_kernel(tc, logits, pred_masks, tgt_masks, offs, out):
@@ -50,9 +51,10 @@ def tile_edlhungarianmatcher_kernel(tc, logits, pred_masks, tgt_masks, offs, out
         tm_ps = [psum.tile([Q, PIECE], F32, name=f"tm_ps{k}") for k in range(PIECES)]
         for k in range(PIECES):
             nc.tensor.matmul(tm_ps[k][:], ones[:], tgt[:, pieces[k]], start=True, stop=True)
-        tm_less_2inter_ps = [psum.tile([Q, PIECE], F32, name=f"tm_less_2inter_ps{k}") for k in range(PIECES)]
-        for k in range(PIECES):
-            nc.tensor.matmul(tm_less_2inter_ps[k][:], weights[:], tgt[:, pieces[k]], start=True, stop=True)
+        last_pieces = [slice(k * LAST_PIECE, (k + 1) * LAST_PIECE) for k in range(N // LAST_PIECE)]
+        tm_less_2inter_ps = [psum.tile([Q, LAST_PIECE], F32, name=f"tm_less_2inter_ps{k}") for k in range(len(last_pieces))]
+        for k, piece in enumerate(last_pieces):
+            nc.tensor.matmul(tm_less_2inter_ps[k][:], weights[:], tgt[:, piece], start=True, stop=True)
         pm = held.tile([Q, 1], F32, name="pm")
         nc.vector.reduce_sum(pm[:], pred[:], axis=AXIS.X)
         pm_plus_1 = held.tile([Q, 1], F32, name="pm_plus_1")
@@ -98,15 +100,15 @@ def tile_edlhungarianmatcher_kernel(tc, logits, pred_masks, tgt_masks, offs, out
                     )
 
         no_dice = held.tile([Q, N], F32, name="no_dice")
-        dice = held.tile([Q, N], F32, name="dice")
-        cost = held.tile([Q, N], F32, name="cost")
-        for k in range(PIECES):
-            piece = pieces[k]
-            nc.vector.scalar_tensor_tensor(
-                dice[:, piece], tm_less_2inter_ps[k][:], pm[:], inv_denom[:, piece], op0=ALU.add, op1=ALU.mult
-            )
+        for piece in pieces:
             nc.vector.scalar_tensor_tensor(
                 no_dice[:, piece], min_sum[:, piece], -2.0, picked[:, piece], op0=ALU.mult, op1=ALU.add
+            )
+        dice = held.tile([Q, N], F32, name="dice")
+        cost = held.tile([Q, N], F32, name="cost")
+        for k, piece in enumerate(last_pieces):
+            nc.vector.scalar_tensor_tensor(
+                dice[:, piece], tm_less_2inter_ps[k][:], pm[:], inv_denom[:, piece], op0=ALU.add, op1=ALU.mult
             )
             nc.vector.tensor_tensor(cost[:, piece], no_dice[:, piece], dice[:, piece], ALU.add)
             queue = nc.sync if k % 2 == 0 else nc.scalar

@@ -51,10 +51,13 @@ def tile_edlhungarianmatcher_kernel(tc, logits, pred_masks, tgt_masks, offs, out
         tm_ps = [psum.tile([Q, PIECE], F32, name=f"tm_ps{k}") for k in range(PIECES)]
         for k in range(PIECES):
             nc.tensor.matmul(tm_ps[k][:], ones[:], tgt[:, pieces[k]], start=True, stop=True)
-        last_pieces = [slice(k * LAST_PIECE, (k + 1) * LAST_PIECE) for k in range(N // LAST_PIECE)]
+        last_starts = list(range(0, N - LAST_PIECE, LAST_PIECE)) + [N - LAST_PIECE, N - LAST_PIECE // 2]
+        last_pieces = [slice(a, b) for a, b in zip(last_starts, last_starts[1:] + [N])]
         tm_less_2inter_ps = [psum.tile([Q, LAST_PIECE], F32, name=f"tm_less_2inter_ps{k}") for k in range(len(last_pieces))]
         for k, piece in enumerate(last_pieces):
-            nc.tensor.matmul(tm_less_2inter_ps[k][:], weights[:], tgt[:, piece], start=True, stop=True)
+            nc.tensor.matmul(
+                tm_less_2inter_ps[k][:, 0 : piece.stop - piece.start], weights[:], tgt[:, piece], start=True, stop=True
+            )
         pm = held.tile([Q, 1], F32, name="pm")
         nc.vector.reduce_sum(pm[:], pred[:], axis=AXIS.X)
         pm_plus_1 = held.tile([Q, 1], F32, name="pm_plus_1")
@@ -108,7 +111,8 @@ def tile_edlhungarianmatcher_kernel(tc, logits, pred_masks, tgt_masks, offs, out
         cost = held.tile([Q, N], F32, name="cost")
         for k, piece in enumerate(last_pieces):
             nc.vector.scalar_tensor_tensor(
-                dice[:, piece], tm_less_2inter_ps[k][:], pm[:], inv_denom[:, piece], op0=ALU.add, op1=ALU.mult
+                dice[:, piece], tm_less_2inter_ps[k][:, 0 : piece.stop - piece.start], pm[:], inv_denom[:, piece],
+                op0=ALU.add, op1=ALU.mult,
             )
             nc.vector.tensor_tensor(cost[:, piece], no_dice[:, piece], dice[:, piece], ALU.add)
             queue = nc.sync if k % 2 == 0 else nc.scalar

@@ -51,9 +51,9 @@ def tile_edlhungarianmatcher_kernel(tc, logits, pred_masks, tgt_masks, offs, out
         tm_ps = [psum.tile([Q, PIECE], F32, name=f"tm_ps{k}") for k in range(PIECES)]
         for k in range(PIECES):
             nc.tensor.matmul(tm_ps[k][:], ones[:], tgt[:, pieces[k]], start=True, stop=True)
-        last_starts = list(range(0, N - LAST_PIECE, LAST_PIECE)) + [N - LAST_PIECE, N - LAST_PIECE // 2]
+        last_starts = [0, N - 2 * LAST_PIECE, N - LAST_PIECE]
         last_pieces = [slice(a, b) for a, b in zip(last_starts, last_starts[1:] + [N])]
-        tm_less_2inter_ps = [psum.tile([Q, LAST_PIECE], F32, name=f"tm_less_2inter_ps{k}") for k in range(len(last_pieces))]
+        tm_less_2inter_ps = [psum.tile([Q, PIECE], F32, name=f"tm_less_2inter_ps{k}") for k in range(len(last_pieces))]
         for k, piece in enumerate(last_pieces):
             nc.tensor.matmul(
                 tm_less_2inter_ps[k][:, 0 : piece.stop - piece.start], weights[:], tgt[:, piece], start=True, stop=True

@@ -13,6 +13,7 @@ PIECES = N // PIECE
 FLOPS = 2 * Q * N * P
 ROWS_PER_LOAD = 2
 LAST_PIECE = 128
+SCALAR_PIXEL = P - 1
 
 
 def tile_edlhungarianmatcher_kernel(tc, logits, pred_masks, tgt_masks, offs, out):
@@ -53,15 +54,32 @@ def tile_edlhungarianmatcher_kernel(tc, logits, pred_masks, tgt_masks, offs, out
             nc.tensor.matmul(tm_ps[k][:], ones[:], tgt[:, pieces[k]], start=True, stop=True)
         last_starts = [0, N - 2 * LAST_PIECE, N - LAST_PIECE]
         last_pieces = [slice(a, b) for a, b in zip(last_starts, last_starts[1:] + [N])]
-        tm_less_2inter_ps = [psum.tile([Q, PIECE], F32, name=f"tm_less_2inter_ps{k}") for k in range(len(last_pieces))]
-        for k, piece in enumerate(last_pieces):
-            nc.tensor.matmul(
-                tm_less_2inter_ps[k][:, 0 : piece.stop - piece.start], weights[:], tgt[:, piece], start=True, stop=True
-            )
         pm = held.tile([Q, 1], F32, name="pm")
         nc.vector.reduce_sum(pm[:], pred[:], axis=AXIS.X)
         pm_plus_1 = held.tile([Q, 1], F32, name="pm_plus_1")
         nc.vector.tensor_scalar_add(pm_plus_1[:], pm[:], 1.0)
+        pm_plus_half = held.tile([Q, 1], F32, name="pm_plus_half")
+        nc.vector.tensor_scalar_add(pm_plus_half[:], pm[:], 0.5)
+        pm_less_quarter = held.tile([Q, 1], F32, name="pm_less_quarter")
+        nc.vector.tensor_scalar_add(pm_less_quarter[:], pm[:], -0.25)
+        inv_root = held.tile([Q, N], F32, name="inv_root")
+        square = held.tile([Q, N], F32, name="square")
+        for k in range(PIECES):
+            piece = pieces[k]
+            nc.scalar.activation(inv_root[:, piece], tm_ps[k][:], ACT.Abs_reciprocal_sqrt, bias=pm_plus_1[:], scale=1.0)
+            nc.scalar.activation(square[:, piece], tm_ps[k][:], ACT.Square, bias=pm_plus_half[:], scale=1.0)
+        numerator_ps = [psum.tile([Q, PIECE], F32, name=f"numerator_ps{k}") for k in range(len(last_pieces))]
+        for k, piece in enumerate(last_pieces):
+            nc.tensor.matmul(
+                numerator_ps[k][:, 0 : piece.stop - piece.start], identity[:], square[:, piece], start=True, stop=False
+            )
+        for k, piece in enumerate(last_pieces):
+            nc.tensor.matmul(
+                numerator_ps[k][:, 0 : piece.stop - piece.start], weights[:], tgt[:, piece], start=False, stop=True
+            )
+        inv_denom = held.tile([Q, N], F32, name="inv_denom")
+        for piece in pieces:
+            nc.scalar.activation(inv_denom[:, piece], inv_root[:, piece], ACT.Square)
 
         neg_max = held.tile([Q, 1], F32, name="neg_max")
         nc.vector.reduce_max(neg_max[:], scores[:], axis=AXIS.X, negate=True)
@@ -73,28 +91,29 @@ def tile_edlhungarianmatcher_kernel(tc, logits, pred_masks, tgt_masks, offs, out
         neg_prob = held.tile([Q, S], F32, name="neg_prob")
         nc.vector.tensor_scalar(neg_prob[:], expd[:], inv_sum[:], -1.0, op0=ALU.mult, op1=ALU.mult)
 
-        inv_root = held.tile([Q, N], F32, name="inv_root")
-        inv_denom = held.tile([Q, N], F32, name="inv_denom")
-        mask_sums = held.tile([Q, N], F32, name="mask_sums")
-        for k in range(PIECES):
-            piece = pieces[k]
-            nc.scalar.activation(inv_root[:, piece], tm_ps[k][:], ACT.Abs_reciprocal_sqrt, bias=pm_plus_1[:], scale=1.0)
-            nc.scalar.activation(inv_denom[:, piece], inv_root[:, piece], ACT.Square)
-            nc.scalar.activation(mask_sums[:, piece], tm_ps[k][:], ACT.Identity, bias=pm[:], scale=1.0)
+        own = pred[:, SCALAR_PIXEL : SCALAR_PIXEL + 1]
+        twice_own = held.tile([Q, 1], F32, name="twice_own")
+        nc.vector.tensor_scalar_mul(twice_own[:], own, 2.0)
+        twice_relu = held.tile([Q, N], F32, name="twice_relu")
+        for piece in pieces:
+            nc.scalar.activation(
+                twice_relu[:, piece], tgt_rows[SCALAR_PIXEL][:, piece], ACT.Relu, bias=twice_own[:], scale=-2.0
+            )
 
         picked = held.tile([Q, N], F32, name="picked")
         for k in range(PIECES):
             piece_offsets = offsets[:, k * (PIECE // 16) : (k + 1) * (PIECE // 16)]
             nc.vector.tensor_tensor(
-                picked[:, pieces[k]], neg_prob[:].indirect(piece_offsets), mask_sums[:, pieces[k]], ALU.add
+                picked[:, pieces[k]], neg_prob[:].indirect(piece_offsets), twice_relu[:, pieces[k]], ALU.add
             )
 
         min_sum = held.tile([Q, N], F32, name="min_sum")
-        for n in range(P):
+        vector_pixels = [n for n in range(P) if n != SCALAR_PIXEL]
+        for n in vector_pixels:
             for piece in pieces:
-                if n == 0:
+                if n == vector_pixels[0]:
                     nc.vector.tensor_scalar(
-                        min_sum[:, piece], tgt_rows[n][:, piece], pred[:, n : n + 1], None, op0=ALU.min
+                        min_sum[:, piece], tgt_rows[n][:, piece], pred[:, n : n + 1], own, op0=ALU.min, op1=ALU.add
                     )
                 else:
                     nc.vector.scalar_tensor_tensor(
@@ -111,7 +130,7 @@ def tile_edlhungarianmatcher_kernel(tc, logits, pred_masks, tgt_masks, offs, out
         cost = held.tile([Q, N], F32, name="cost")
         for k, piece in enumerate(last_pieces):
             nc.vector.scalar_tensor_tensor(
-                dice[:, piece], tm_less_2inter_ps[k][:, 0 : piece.stop - piece.start], pm[:], inv_denom[:, piece],
+                dice[:, piece], numerator_ps[k][:, 0 : piece.stop - piece.start], pm_less_quarter[:], inv_denom[:, piece],
                 op0=ALU.add, op1=ALU.mult,
             )
             nc.vector.tensor_tensor(cost[:, piece], no_dice[:, piece], dice[:, piece], ALU.add)

@@ -11,7 +11,7 @@ Q, S, N, P = 128, 256, 512, 8
 PIECE = S
 PIECES = N // PIECE
 FLOPS = 2 * Q * N * P
-ROWS_PER_LOAD = 2
+ROWS_OF_LOADS = [4, 2, 2]
 LAST_PIECE = 128
 SCALAR_PIXEL = P - 1
 
@@ -26,11 +26,12 @@ def tile_edlhungarianmatcher_kernel(tc, logits, pred_masks, tgt_masks, offs, out
         tgt = held.tile([P, N], F32, name="tgt")
         nc.sync.dma_start(tgt[:], tgt_masks)
         tgt_rows = []
-        for first in range(0, P, ROWS_PER_LOAD):
-            rows = held.tile([Q, ROWS_PER_LOAD * N], F32, name=f"tgt_rows{first}")
-            source = tgt_masks[first : first + ROWS_PER_LOAD, :].rearrange("n j -> (n j)")
+        for count in ROWS_OF_LOADS:
+            first = len(tgt_rows)
+            rows = held.tile([Q, count * N], F32, name=f"tgt_rows{first}")
+            source = tgt_masks[first : first + count, :].rearrange("n j -> (n j)")
             nc.sync.dma_start(rows[:], source.partition_broadcast(Q))
-            for r in range(ROWS_PER_LOAD):
+            for r in range(count):
                 tgt_rows.append(rows[:, r * N : (r + 1) * N])
         offsets = held.tile([Q, N // 16], U16, name="offsets")
         nc.sync.dma_start(offsets[:], offs)

@@ -40,9 +40,6 @@ def tile_edlhungarianmatcher_kernel(tc, logits, pred_masks, tgt_masks, offs, out
         nc.gpsimd.memset(ones[:], 1.0)
         identity = held.tile([Q, Q], F32, name="identity")
         make_identity(nc, identity[:])
-        scratch = held.tile([Q, 1], F32, name="scratch")
-        nc.vector.memset(scratch[:], 0.0)
-        nc.scalar.activation(scratch[:], scratch[:], ACT.Exp)
 
         pieces = [slice(k * PIECE, (k + 1) * PIECE) for k in range(PIECES)]
 

import concourse.mybir as mybir
from concourse.masks import make_identity

F32 = mybir.dt.float32
U16 = mybir.dt.uint16
ALU = mybir.AluOpType
ACT = mybir.ActivationFunctionType
AXIS = mybir.AxisListType

Q, S, N, P = 128, 256, 512, 8
PIECE = S
PIECES = N // PIECE
FLOPS = 2 * Q * N * P
ROWS_OF_LOADS = [4, 2, 2]
LAST_PIECE = 128
SCALAR_PIXEL = P - 1


def tile_edlhungarianmatcher_kernel(tc, logits, pred_masks, tgt_masks, offs, out):
    nc = tc.nc
    with tc.tile_pool(name="held", bufs=1) as held, tc.psum_pool(name="psum", bufs=1) as psum:
        scores = held.tile([Q, S], F32, name="scores")
        nc.scalar.dma_start(scores[:], logits)
        pred = held.tile([Q, P], F32, name="pred")
        nc.sync.dma_start(pred[:], pred_masks)
        tgt = held.tile([P, N], F32, name="tgt")
        nc.sync.dma_start(tgt[:], tgt_masks)
        tgt_rows = []
        for count in ROWS_OF_LOADS:
            first = len(tgt_rows)
            rows = held.tile([Q, count * N], F32, name=f"tgt_rows{first}")
            source = tgt_masks[first : first + count, :].rearrange("n j -> (n j)")
            nc.sync.dma_start(rows[:], source.partition_broadcast(Q))
            for r in range(count):
                tgt_rows.append(rows[:, r * N : (r + 1) * N])
        offsets = held.tile([Q, N // 16], U16, name="offsets")
        nc.sync.dma_start(offsets[:], offs)

        ones = held.tile([P, Q], F32, name="ones")
        nc.gpsimd.memset(ones[:], 1.0)
        identity = held.tile([Q, Q], F32, name="identity")
        make_identity(nc, identity[:])

        pieces = [slice(k * PIECE, (k + 1) * PIECE) for k in range(PIECES)]

        pred_t_ps = psum.tile([P, Q], F32, name="pred_t_ps")
        nc.tensor.transpose(pred_t_ps[:], pred[:], identity[:])
        weights = held.tile([P, Q], F32, name="weights")
        nc.scalar.activation(weights[:], pred_t_ps[:], ACT.Identity, bias=1.0, scale=-2.0)
        tm_ps = [psum.tile([Q, PIECE], F32, name=f"tm_ps{k}") for k in range(PIECES)]
        for k in range(PIECES):
            nc.tensor.matmul(tm_ps[k][:], ones[:], tgt[:, pieces[k]], start=True, stop=True)
        last_starts = [0, N - 2 * LAST_PIECE, N - LAST_PIECE]
        last_pieces = [slice(a, b) for a, b in zip(last_starts, last_starts[1:] + [N])]
        pm = held.tile([Q, 1], F32, name="pm")
        nc.vector.reduce_sum(pm[:], pred[:], axis=AXIS.X)
        pm_plus_1 = held.tile([Q, 1], F32, name="pm_plus_1")
        nc.vector.tensor_scalar_add(pm_plus_1[:], pm[:], 1.0)
        pm_plus_half = held.tile([Q, 1], F32, name="pm_plus_half")
        nc.vector.tensor_scalar_add(pm_plus_half[:], pm[:], 0.5)
        pm_less_quarter = held.tile([Q, 1], F32, name="pm_less_quarter")
        nc.vector.tensor_scalar_add(pm_less_quarter[:], pm[:], -0.25)
        inv_root = held.tile([Q, N], F32, name="inv_root")
        square = held.tile([Q, N], F32, name="square")
        for k in range(PIECES):
            piece = pieces[k]
            nc.scalar.activation(inv_root[:, piece], tm_ps[k][:], ACT.Abs_reciprocal_sqrt, bias=pm_plus_1[:], scale=1.0)
            nc.scalar.activation(square[:, piece], tm_ps[k][:], ACT.Square, bias=pm_plus_half[:], scale=1.0)
        numerator_ps = [psum.tile([Q, PIECE], F32, name=f"numerator_ps{k}") for k in range(len(last_pieces))]
        for k, piece in enumerate(last_pieces):
            nc.tensor.matmul(
                numerator_ps[k][:, 0 : piece.stop - piece.start], identity[:], square[:, piece], start=True, stop=False
            )
        for k, piece in enumerate(last_pieces):
            nc.tensor.matmul(
                numerator_ps[k][:, 0 : piece.stop - piece.start], weights[:], tgt[:, piece], start=False, stop=True
            )
        inv_denom = held.tile([Q, N], F32, name="inv_denom")
        for piece in pieces:
            nc.scalar.activation(inv_denom[:, piece], inv_root[:, piece], ACT.Square)

        neg_max = held.tile([Q, 1], F32, name="neg_max")
        nc.vector.reduce_max(neg_max[:], scores[:], axis=AXIS.X, negate=True)
        expd = held.tile([Q, S], F32, name="expd")
        exp_sum = held.tile([Q, 1], F32, name="exp_sum")
        nc.scalar.activation(expd[:], scores[:], ACT.Exp, bias=neg_max[:], scale=1.0, accum_out=exp_sum[:])
        inv_sum = held.tile([Q, 1], F32, name="inv_sum")
        nc.vector.reciprocal(inv_sum[:], exp_sum[:])
        neg_prob = held.tile([Q, S], F32, name="neg_prob")
        nc.vector.tensor_scalar(neg_prob[:], expd[:], inv_sum[:], -1.0, op0=ALU.mult, op1=ALU.mult)

        own = pred[:, SCALAR_PIXEL : SCALAR_PIXEL + 1]
        twice_own = held.tile([Q, 1], F32, name="twice_own")
        nc.vector.tensor_scalar_mul(twice_own[:], own, 2.0)
        twice_relu = held.tile([Q, N], F32, name="twice_relu")
        for piece in pieces:
            nc.scalar.activation(
                twice_relu[:, piece], tgt_rows[SCALAR_PIXEL][:, piece], ACT.Relu, bias=twice_own[:], scale=-2.0
            )

        picked = held.tile([Q, N], F32, name="picked")
        for k in range(PIECES):
            piece_offsets = offsets[:, k * (PIECE // 16) : (k + 1) * (PIECE // 16)]
            nc.vector.tensor_tensor(
                picked[:, pieces[k]], neg_prob[:].indirect(piece_offsets), twice_relu[:, pieces[k]], ALU.add
            )

        min_sum = held.tile([Q, N], F32, name="min_sum")
        vector_pixels = [n for n in range(P) if n != SCALAR_PIXEL]
        for n in vector_pixels:
            for piece in pieces:
                if n == vector_pixels[0]:
                    nc.vector.tensor_scalar(
                        min_sum[:, piece], tgt_rows[n][:, piece], pred[:, n : n + 1], own, op0=ALU.min, op1=ALU.add
                    )
                else:
                    nc.vector.scalar_tensor_tensor(
                        min_sum[:, piece], tgt_rows[n][:, piece], pred[:, n : n + 1], min_sum[:, piece],
                        op0=ALU.min, op1=ALU.add,
                    )

        no_dice = held.tile([Q, N], F32, name="no_dice")
        for piece in pieces:
            nc.vector.scalar_tensor_tensor(
                no_dice[:, piece], min_sum[:, piece], -2.0, picked[:, piece], op0=ALU.mult, op1=ALU.add
            )
        dice = held.tile([Q, N], F32, name="dice")
        cost = held.tile([Q, N], F32, name="cost")
        for k, piece in enumerate(last_pieces):
            nc.vector.scalar_tensor_tensor(
                dice[:, piece], numerator_ps[k][:, 0 : piece.stop - piece.start], pm_less_quarter[:], inv_denom[:, piece],
                op0=ALU.add, op1=ALU.mult,
            )
            nc.vector.tensor_tensor(cost[:, piece], no_dice[:, piece], dice[:, piece], ALU.add)
            queue = nc.sync if k % 2 == 0 else nc.scalar
            queue.dma_start(out[:, piece], cost[:, piece])
